import numpy as np
import ml_dtypes

BF16 = ml_dtypes.bfloat16


def bf(x):
    return np.asarray(x, np.float32).astype(BF16)


def f32(x):
    return np.asarray(x, np.float32)


def f64(x):
    return np.asarray(x).astype(np.float64)


def striped(idx):
    return np.tile(idx.reshape(-1, 16).T, (8, 1))


C, K, D, R, S, N = 128, 4, 128, 8, 512, 256


def setup_inputs():
    mix = np.random.standard_normal((R, D))
    cent = (np.random.standard_normal((C, K, R)) @ mix) / np.sqrt(R * D) * np.random.uniform(1.0, 4.0, (C, K, 1))
    cod = mix.T @ np.random.standard_normal((R, N))
    cod = cod / np.sqrt((cod**2).sum(axis=0, keepdims=True))
    return {"base": f32(np.random.uniform(0.0, 2.0, (C, S))), "codes": bf(cod), "centroids": f32(cent), "offs": striped(np.random.permutation(S)[:N])}


def reference(base, codes, centroids, offs):
    idx = offs[:16].T.reshape(-1)
    cen = f64(centroids)
    cn = cen / np.sqrt((cen**2).sum(axis=-1, keepdims=True))
    sim = np.einsum("ckd,dn->ckn", cn, f64(codes))
    mx = sim.max(axis=1)
    out = f64(base).copy()
    out[:, idx] = 1.0 + (-mx)
    return out

@@ -1,0 +1,54 @@
+import concourse.mybir as mybir
+from concourse.masks import make_identity
+
+C, K, D, S, N = 128, 4, 128, 512, 256
+FLOPS = 2 * C * K * D * N
+
+F32, BF16, U16 = mybir.dt.float32, mybir.dt.bfloat16, mybir.dt.uint16
+ALU = mybir.AluOpType
+ACT = mybir.ActivationFunctionType
+
+
+def tile_cosinecodebook_kernel(tc, base, codes, centroids, offs, out):
+    nc = tc.nc
+    with tc.tile_pool(name="held", bufs=1) as held, tc.psum_pool(name="psum", bufs=1) as psum:
+        offsets = held.tile([C, N // 16], U16, name="offsets")
+        nc.sync.dma_start(offsets[:], offs)
+        cen = held.tile([C, K, D], F32, name="cen")
+        nc.sync.dma_start(cen[:], centroids)
+        codes_sb = held.tile([D, N], BF16, name="codes_sb")
+        nc.scalar.dma_start(codes_sb[:], codes)
+        bank = held.tile([C, S], F32, name="bank")
+        nc.scalar.dma_start(bank[:], base)
+
+        identity = held.tile([C, C], F32, name="identity")
+        make_identity(nc, identity[:])
+        ones = held.tile([C, N], F32, name="ones")
+        nc.gpsimd.memset(ones[:], 1.0)
+
+        squares = held.tile([C, D], F32, name="squares")
+        sumsq = held.tile([C, K], F32, name="sumsq")
+        for k in range(K):
+            nc.scalar.activation(squares[:], cen[:, k, :], ACT.Square, accum_out=sumsq[:, k : k + 1])
+        length = held.tile([C, K], F32, name="length")
+        nc.scalar.activation(length[:], sumsq[:], ACT.Sqrt)
+        inv_length = held.tile([C, K], F32, name="inv_length")
+        nc.vector.reciprocal(inv_length[:], length[:])
+
+        neg_max = held.tile([C, N], F32, name="neg_max")
+        for k in range(K):
+            cen_t = psum.tile([D, C], F32, name=f"cen_t{k}")
+            nc.tensor.transpose(cen_t[:], cen[:, k, :], identity[:])
+            neg_cen_t = held.tile([D, C], BF16, name=f"neg_cen_t{k}")
+            nc.vector.tensor_scalar(neg_cen_t[:], cen_t[:], -1.0, None, op0=ALU.mult)
+            neg_dot = psum.tile([C, N], F32, name=f"neg_dot{k}")
+            nc.tensor.matmul(neg_dot[:], neg_cen_t[:], codes_sb[:], start=True, stop=True)
+            if k == 0:
+                nc.vector.tensor_scalar(neg_max[:], neg_dot[:], inv_length[:, 0:1], None, op0=ALU.mult)
+            else:
+                nc.vector.scalar_tensor_tensor(
+                    neg_max[:], neg_dot[:], inv_length[:, k : k + 1], neg_max[:], op0=ALU.mult, op1=ALU.min
+                )
+
+        nc.vector.tensor_tensor(bank[:].indirect(offsets[:]), ones[:], neg_max[:], ALU.add)
+        nc.sync.dma_start(out, bank[:])

@@ -12,43 +12,52 @@ ACT = mybir.ActivationFunctionType
 def tile_cosinecodebook_kernel(tc, base, codes, centroids, offs, out):
     nc = tc.nc
     with tc.tile_pool(name="held", bufs=1) as held, tc.psum_pool(name="psum", bufs=1) as psum:
-        offsets = held.tile([C, N // 16], U16, name="offsets")
-        nc.sync.dma_start(offsets[:], offs)
-        cen = held.tile([C, K, D], F32, name="cen")
-        nc.sync.dma_start(cen[:], centroids)
+        cen = [held.tile([C, D], F32, name=f"cen{k}") for k in range(K)]
+        nc.sync.dma_start(cen[0][:], centroids[:, 0, :])
+        nc.scalar.dma_start(cen[1][:], centroids[:, 1, :])
+        nc.sync.dma_start(cen[2][:], centroids[:, 2, :])
+        nc.scalar.dma_start(cen[3][:], centroids[:, 3, :])
         codes_sb = held.tile([D, N], BF16, name="codes_sb")
-        nc.scalar.dma_start(codes_sb[:], codes)
+        nc.sync.dma_start(codes_sb[:], codes)
         bank = held.tile([C, S], F32, name="bank")
         nc.scalar.dma_start(bank[:], base)
+        offsets = held.tile([C, N // 16], U16, name="offsets")
+        nc.sync.dma_start(offsets[:], offs)
 
         identity = held.tile([C, C], F32, name="identity")
         make_identity(nc, identity[:])
         ones = held.tile([C, N], F32, name="ones")
-        nc.gpsimd.memset(ones[:], 1.0)
+        nc.vector.memset(ones[:], 1.0)
+
+        warm = held.tile([C, 1], F32, name="warm")
+        nc.scalar.activation(warm[:], ones[:, 0:1], ACT.Abs_reciprocal_sqrt)
+
+        neg_cen_t = [held.tile([D, C], BF16, name=f"neg_cen_t{k}") for k in range(K)]
+        for k in range(K):
+            cen_t = psum.tile([D, C], F32, name=f"cen_t{k}")
+            nc.tensor.transpose(cen_t[:], cen[k][:], identity[:])
+            nc.vector.tensor_scalar(neg_cen_t[k][:], cen_t[:], -1.0, None, op0=ALU.mult)
 
         squares = held.tile([C, D], F32, name="squares")
         sumsq = held.tile([C, K], F32, name="sumsq")
         for k in range(K):
-            nc.scalar.activation(squares[:], cen[:, k, :], ACT.Square, accum_out=sumsq[:, k : k + 1])
-        length = held.tile([C, K], F32, name="length")
-        nc.scalar.activation(length[:], sumsq[:], ACT.Sqrt)
+            nc.scalar.activation(squares[:], cen[k][:], ACT.Square, accum_out=sumsq[:, k : k + 1])
         inv_length = held.tile([C, K], F32, name="inv_length")
-        nc.vector.reciprocal(inv_length[:], length[:])
+        nc.scalar.activation(inv_length[:], sumsq[:], ACT.Abs_reciprocal_sqrt)
 
-        neg_max = held.tile([C, N], F32, name="neg_max")
+        neg_dot = [psum.tile([C, N], F32, name=f"neg_dot{k}") for k in range(K)]
         for k in range(K):
-            cen_t = psum.tile([D, C], F32, name=f"cen_t{k}")
-            nc.tensor.transpose(cen_t[:], cen[:, k, :], identity[:])
-            neg_cen_t = held.tile([D, C], BF16, name=f"neg_cen_t{k}")
-            nc.vector.tensor_scalar(neg_cen_t[:], cen_t[:], -1.0, None, op0=ALU.mult)
-            neg_dot = psum.tile([C, N], F32, name=f"neg_dot{k}")
-            nc.tensor.matmul(neg_dot[:], neg_cen_t[:], codes_sb[:], start=True, stop=True)
-            if k == 0:
-                nc.vector.tensor_scalar(neg_max[:], neg_dot[:], inv_length[:, 0:1], None, op0=ALU.mult)
-            else:
-                nc.vector.scalar_tensor_tensor(
-                    neg_max[:], neg_dot[:], inv_length[:, k : k + 1], neg_max[:], op0=ALU.mult, op1=ALU.min
-                )
+            nc.tensor.matmul(neg_dot[k][:], neg_cen_t[k][:], codes_sb[:], start=True, stop=True)
+
+        partial = [held.tile([C, N], F32, name=f"partial{h}") for h in range(2)]
+        for h in range(2):
+            nc.scalar.activation(partial[h][:], neg_dot[h][:], ACT.Copy, scale=inv_length[:, h : h + 1])
+        for h in range(2):
+            nc.vector.scalar_tensor_tensor(
+                partial[h][:], neg_dot[2 + h][:], inv_length[:, 2 + h : 3 + h], partial[h][:], op0=ALU.mult, op1=ALU.min
+            )
+        neg_max = held.tile([C, N], F32, name="neg_max")
+        nc.vector.tensor_tensor(neg_max[:], partial[0][:], partial[1][:], ALU.min)
 
         nc.vector.tensor_tensor(bank[:].indirect(offsets[:]), ones[:], neg_max[:], ALU.add)
         nc.sync.dma_start(out, bank[:])

@@ -60,4 +60,5 @@ def tile_cosinecodebook_kernel(tc, base, codes, centroids, offs, out):
         nc.vector.tensor_tensor(neg_max[:], partial[0][:], partial[1][:], ALU.min)
 
         nc.vector.tensor_tensor(bank[:].indirect(offsets[:]), ones[:], neg_max[:], ALU.add)
-        nc.sync.dma_start(out, bank[:])
+        nc.sync.dma_start(out[:, : S // 2], bank[:, : S // 2])
+        nc.scalar.dma_start(out[:, S // 2 :], bank[:, S // 2 :])

@@ -19,10 +19,10 @@ def tile_cosinecodebook_kernel(tc, base, codes, centroids, offs, out):
         nc.scalar.dma_start(cen[3][:], centroids[:, 3, :])
         codes_sb = held.tile([D, N], BF16, name="codes_sb")
         nc.sync.dma_start(codes_sb[:], codes)
-        bank = held.tile([C, S], F32, name="bank")
-        nc.scalar.dma_start(bank[:], base)
         offsets = held.tile([C, N // 16], U16, name="offsets")
         nc.sync.dma_start(offsets[:], offs)
+        bank = held.tile([C, S], F32, name="bank")
+        nc.sync.dma_start(bank[:], base)
 
         identity = held.tile([C, C], F32, name="identity")
         make_identity(nc, identity[:])
@@ -60,5 +60,4 @@ def tile_cosinecodebook_kernel(tc, base, codes, centroids, offs, out):
         nc.vector.tensor_tensor(neg_max[:], partial[0][:], partial[1][:], ALU.min)
 
         nc.vector.tensor_tensor(bank[:].indirect(offsets[:]), ones[:], neg_max[:], ALU.add)
-        nc.sync.dma_start(out[:, : S // 2], bank[:, : S // 2])
-        nc.scalar.dma_start(out[:, S // 2 :], bank[:, S // 2 :])
+        nc.sync.dma_start(out, bank[:])

@@ -14,9 +14,9 @@ def tile_cosinecodebook_kernel(tc, base, codes, centroids, offs, out):
     with tc.tile_pool(name="held", bufs=1) as held, tc.psum_pool(name="psum", bufs=1) as psum:
         cen = [held.tile([C, D], F32, name=f"cen{k}") for k in range(K)]
         nc.sync.dma_start(cen[0][:], centroids[:, 0, :])
-        nc.scalar.dma_start(cen[1][:], centroids[:, 1, :])
+        nc.sync.dma_start(cen[1][:], centroids[:, 1, :])
         nc.sync.dma_start(cen[2][:], centroids[:, 2, :])
-        nc.scalar.dma_start(cen[3][:], centroids[:, 3, :])
+        nc.sync.dma_start(cen[3][:], centroids[:, 3, :])
         codes_sb = held.tile([D, N], BF16, name="codes_sb")
         nc.sync.dma_start(codes_sb[:], codes)
         offsets = held.tile([C, N // 16], U16, name="offsets")

@@ -32,16 +32,22 @@ def tile_cosinecodebook_kernel(tc, base, codes, centroids, offs, out):
         warm = held.tile([C, 1], F32, name="warm")
         nc.scalar.activation(warm[:], ones[:, 0:1], ACT.Abs_reciprocal_sqrt)
 
+        sumsq = held.tile([C, K], F32, name="sumsq")
+        squares_v = held.tile([C, D], F32, name="squares_v")
+        squares_s = held.tile([C, D], F32, name="squares_s")
+        for k in (0, 1):
+            nc.vector.scalar_tensor_tensor(
+                squares_v[:], cen[k][:], 1.0, cen[k][:], op0=ALU.mult, op1=ALU.mult, accum_out=sumsq[:, k : k + 1]
+            )
+        for k in (2, 3):
+            nc.scalar.activation(squares_s[:], cen[k][:], ACT.Square, accum_out=sumsq[:, k : k + 1])
+
         neg_cen_t = [held.tile([D, C], BF16, name=f"neg_cen_t{k}") for k in range(K)]
         for k in range(K):
             cen_t = psum.tile([D, C], F32, name=f"cen_t{k}")
             nc.tensor.transpose(cen_t[:], cen[k][:], identity[:])
             nc.vector.tensor_scalar(neg_cen_t[k][:], cen_t[:], -1.0, None, op0=ALU.mult)
 
-        squares = held.tile([C, D], F32, name="squares")
-        sumsq = held.tile([C, K], F32, name="sumsq")
-        for k in range(K):
-            nc.scalar.activation(squares[:], cen[k][:], ACT.Square, accum_out=sumsq[:, k : k + 1])
         inv_length = held.tile([C, K], F32, name="inv_length")
         nc.scalar.activation(inv_length[:], sumsq[:], ACT.Abs_reciprocal_sqrt)
 

@@ -56,14 +56,20 @@ def tile_cosinecodebook_kernel(tc, base, codes, centroids, offs, out):
             nc.tensor.matmul(neg_dot[k][:], neg_cen_t[k][:], codes_sb[:], start=True, stop=True)
 
         partial = [held.tile([C, N], F32, name=f"partial{h}") for h in range(2)]
+        folded = [held.tile([C, N], F32, name=f"folded{h}") for h in range(2)]
+        neg_max = held.tile([C, N], F32, name="neg_max")
         for h in range(2):
             nc.scalar.activation(partial[h][:], neg_dot[h][:], ACT.Copy, scale=inv_length[:, h : h + 1])
-        for h in range(2):
+        nc.vector.scalar_tensor_tensor(
+            folded[0][:], neg_dot[2][:], inv_length[:, 2:3], partial[0][:], op0=ALU.mult, op1=ALU.min
+        )
+        pieces = [slice(0, N // 2), slice(N // 2, N)]
+        for piece in pieces:
             nc.vector.scalar_tensor_tensor(
-                partial[h][:], neg_dot[2 + h][:], inv_length[:, 2 + h : 3 + h], partial[h][:], op0=ALU.mult, op1=ALU.min
+                folded[1][:, piece], neg_dot[3][:, piece], inv_length[:, 3:4], partial[1][:, piece], op0=ALU.mult, op1=ALU.min
             )
-        neg_max = held.tile([C, N], F32, name="neg_max")
-        nc.vector.tensor_tensor(neg_max[:], partial[0][:], partial[1][:], ALU.min)
+        for piece in pieces:
+            nc.vector.tensor_tensor(neg_max[:, piece], folded[0][:, piece], folded[1][:, piece], ALU.min)
 
         nc.vector.tensor_tensor(bank[:].indirect(offsets[:]), ones[:], neg_max[:], ALU.add)
         nc.sync.dma_start(out, bank[:])

@@ -27,10 +27,12 @@ def tile_cosinecodebook_kernel(tc, base, codes, centroids, offs, out):
         identity = held.tile([C, C], F32, name="identity")
         make_identity(nc, identity[:])
         ones = held.tile([C, N], F32, name="ones")
-        nc.vector.memset(ones[:], 1.0)
+        nc.gpsimd.memset(ones[:], 1.0)
 
+        warm_in = held.tile([C, 1], F32, name="warm_in")
+        nc.vector.memset(warm_in[:], 1.0)
         warm = held.tile([C, 1], F32, name="warm")
-        nc.scalar.activation(warm[:], ones[:, 0:1], ACT.Abs_reciprocal_sqrt)
+        nc.scalar.activation(warm[:], warm_in[:], ACT.Abs_reciprocal_sqrt)
 
         sumsq = held.tile([C, K], F32, name="sumsq")
         squares_v = held.tile([C, D], F32, name="squares_v")

@@ -34,44 +34,49 @@ def tile_cosinecodebook_kernel(tc, base, codes, centroids, offs, out):
         warm = held.tile([C, 1], F32, name="warm")
         nc.scalar.activation(warm[:], warm_in[:], ACT.Abs_reciprocal_sqrt)
 
-        sumsq = held.tile([C, K], F32, name="sumsq")
+        sumsq_v = [held.tile([C, 1], F32, name=f"sumsq_v{k}") for k in (0, 1)]
+        sumsq_s = held.tile([C, 2], F32, name="sumsq_s")
         squares_v = held.tile([C, D], F32, name="squares_v")
         squares_s = held.tile([C, D], F32, name="squares_s")
         for k in (0, 1):
             nc.vector.scalar_tensor_tensor(
-                squares_v[:], cen[k][:], 1.0, cen[k][:], op0=ALU.mult, op1=ALU.mult, accum_out=sumsq[:, k : k + 1]
+                squares_v[:], cen[k][:], 1.0, cen[k][:], op0=ALU.mult, op1=ALU.mult, accum_out=sumsq_v[k][:]
             )
         for k in (2, 3):
-            nc.scalar.activation(squares_s[:], cen[k][:], ACT.Square, accum_out=sumsq[:, k : k + 1])
+            nc.scalar.activation(squares_s[:], cen[k][:], ACT.Square, accum_out=sumsq_s[:, k - 2 : k - 1])
 
         neg_cen_t = [held.tile([D, C], BF16, name=f"neg_cen_t{k}") for k in range(K)]
         for k in range(K):
-            cen_t = psum.tile([D, C], F32, name=f"cen_t{k}")
+            cen_t = psum.tile([D, C], F32, name=f"cen_t{k}", tag=f"bank{k}")
             nc.tensor.transpose(cen_t[:], cen[k][:], identity[:])
             nc.vector.tensor_scalar(neg_cen_t[k][:], cen_t[:], -1.0, None, op0=ALU.mult)
 
-        inv_length = held.tile([C, K], F32, name="inv_length")
-        nc.scalar.activation(inv_length[:], sumsq[:], ACT.Abs_reciprocal_sqrt)
+        inv_length_0 = held.tile([C, 1], F32, name="inv_length_0", tag="inv_length_first")
+        nc.scalar.activation(inv_length_0[:], sumsq_v[0][:], ACT.Abs_reciprocal_sqrt)
+        inv_length_1 = held.tile([C, 1], F32, name="inv_length_1")
+        nc.scalar.activation(inv_length_1[:], sumsq_v[1][:], ACT.Abs_reciprocal_sqrt)
 
-        neg_dot = [psum.tile([C, N], F32, name=f"neg_dot{k}") for k in range(K)]
-        for k in range(K):
-            nc.tensor.matmul(neg_dot[k][:], neg_cen_t[k][:], codes_sb[:], start=True, stop=True)
+        halves = [slice(0, N // 2), slice(N // 2, N)]
+        neg_dot = [
+            [psum.tile([C, N // 2], F32, name=f"neg_dot{k}{h}", tag=f"bank{(2 * k + h + 4) % 8}") for h in range(2)]
+            for k in range(K)
+        ]
+        for k, h in ((0, 0), (1, 0), (0, 1), (1, 1), (2, 0), (2, 1), (3, 0), (3, 1)):
+            nc.tensor.matmul(neg_dot[k][h][:], neg_cen_t[k][:], codes_sb[:, halves[h]], start=True, stop=True)
 
-        partial = [held.tile([C, N], F32, name=f"partial{h}") for h in range(2)]
-        folded = [held.tile([C, N], F32, name=f"folded{h}") for h in range(2)]
-        neg_max = held.tile([C, N], F32, name="neg_max")
+        so_far = [held.tile([C, N], F32, name=f"so_far{k}") for k in range(K)]
         for h in range(2):
-            nc.scalar.activation(partial[h][:], neg_dot[h][:], ACT.Copy, scale=inv_length[:, h : h + 1])
-        nc.vector.scalar_tensor_tensor(
-            folded[0][:], neg_dot[2][:], inv_length[:, 2:3], partial[0][:], op0=ALU.mult, op1=ALU.min
-        )
-        pieces = [slice(0, N // 2), slice(N // 2, N)]
-        for piece in pieces:
-            nc.vector.scalar_tensor_tensor(
-                folded[1][:, piece], neg_dot[3][:, piece], inv_length[:, 3:4], partial[1][:, piece], op0=ALU.mult, op1=ALU.min
-            )
-        for piece in pieces:
-            nc.vector.tensor_tensor(neg_max[:, piece], folded[0][:, piece], folded[1][:, piece], ALU.min)
+            nc.scalar.activation(so_far[0][:, halves[h]], neg_dot[0][h][:], ACT.Copy, scale=inv_length_0[:])
+        inv_length_23 = held.tile([C, 2], F32, name="inv_length_23", tag="inv_length_first")
+        nc.scalar.activation(inv_length_23[:], sumsq_s[:], ACT.Abs_reciprocal_sqrt)
+        inv_length = {1: inv_length_1[:], 2: inv_length_23[:, 0:1], 3: inv_length_23[:, 1:2]}
+        for k in range(1, K):
+            for h in range(2):
+                nc.vector.scalar_tensor_tensor(
+                    so_far[k][:, halves[h]], neg_dot[k][h][:], inv_length[k], so_far[k - 1][:, halves[h]],
+                    op0=ALU.mult, op1=ALU.min,
+                )
+        neg_max = so_far[K - 1]
 
         nc.vector.tensor_tensor(bank[:].indirect(offsets[:]), ones[:], neg_max[:], ALU.add)
         nc.sync.dma_start(out, bank[:])

@@ -64,16 +64,22 @@ def tile_cosinecodebook_kernel(tc, base, codes, centroids, offs, out):
         for k, h in ((0, 0), (1, 0), (0, 1), (1, 1), (2, 0), (2, 1), (3, 0), (3, 1)):
             nc.tensor.matmul(neg_dot[k][h][:], neg_cen_t[k][:], codes_sb[:, halves[h]], start=True, stop=True)
 
+        Q = N // 4
         so_far = [held.tile([C, N], F32, name=f"so_far{k}") for k in range(K)]
-        for h in range(2):
-            nc.scalar.activation(so_far[0][:, halves[h]], neg_dot[0][h][:], ACT.Copy, scale=inv_length_0[:])
+        for q in range(4):
+            in_half = slice(q % 2 * Q, (q % 2 + 1) * Q)
+            nc.scalar.activation(
+                so_far[0][:, q * Q : (q + 1) * Q], neg_dot[0][q // 2][:, in_half], ACT.Copy, scale=inv_length_0[:]
+            )
         inv_length_23 = held.tile([C, 2], F32, name="inv_length_23", tag="inv_length_first")
         nc.scalar.activation(inv_length_23[:], sumsq_s[:], ACT.Abs_reciprocal_sqrt)
         inv_length = {1: inv_length_1[:], 2: inv_length_23[:, 0:1], 3: inv_length_23[:, 1:2]}
         for k in range(1, K):
-            for h in range(2):
+            for q in range(4):
+                quarter = slice(q * Q, (q + 1) * Q)
+                in_half = slice(q % 2 * Q, (q % 2 + 1) * Q)
                 nc.vector.scalar_tensor_tensor(
-                    so_far[k][:, halves[h]], neg_dot[k][h][:], inv_length[k], so_far[k - 1][:, halves[h]],
+                    so_far[k][:, quarter], neg_dot[k][q // 2][:, in_half], inv_length[k], so_far[k - 1][:, quarter],
                     op0=ALU.mult, op1=ALU.min,
                 )
         neg_max = so_far[K - 1]

@@ -36,11 +36,11 @@ def tile_cosinecodebook_kernel(tc, base, codes, centroids, offs, out):
 
         sumsq_v = [held.tile([C, 1], F32, name=f"sumsq_v{k}") for k in (0, 1)]
         sumsq_s = held.tile([C, 2], F32, name="sumsq_s")
-        squares_v = held.tile([C, D], F32, name="squares_v")
+        squares_v = [held.tile([C, D], F32, name=f"squares_v{k}") for k in (0, 1)]
         squares_s = held.tile([C, D], F32, name="squares_s")
         for k in (0, 1):
             nc.vector.scalar_tensor_tensor(
-                squares_v[:], cen[k][:], 1.0, cen[k][:], op0=ALU.mult, op1=ALU.mult, accum_out=sumsq_v[k][:]
+                squares_v[k][:], cen[k][:], 1.0, cen[k][:], op0=ALU.mult, op1=ALU.mult, accum_out=sumsq_v[k][:]
             )
         for k in (2, 3):
             nc.scalar.activation(squares_s[:], cen[k][:], ACT.Square, accum_out=sumsq_s[:, k - 2 : k - 1])

@@ -34,52 +34,47 @@ def tile_cosinecodebook_kernel(tc, base, codes, centroids, offs, out):
         warm = held.tile([C, 1], F32, name="warm")
         nc.scalar.activation(warm[:], warm_in[:], ACT.Abs_reciprocal_sqrt)
 
-        sumsq_v = [held.tile([C, 1], F32, name=f"sumsq_v{k}") for k in (0, 1)]
-        sumsq_s = held.tile([C, 2], F32, name="sumsq_s")
-        squares_v = [held.tile([C, D], F32, name=f"squares_v{k}") for k in (0, 1)]
-        squares_s = held.tile([C, D], F32, name="squares_s")
-        for k in (0, 1):
-            nc.vector.scalar_tensor_tensor(
-                squares_v[k][:], cen[k][:], 1.0, cen[k][:], op0=ALU.mult, op1=ALU.mult, accum_out=sumsq_v[k][:]
-            )
-        for k in (2, 3):
-            nc.scalar.activation(squares_s[:], cen[k][:], ACT.Square, accum_out=sumsq_s[:, k - 2 : k - 1])
+        sumsq_0 = held.tile([C, 1], F32, name="sumsq_0")
+        sumsq_123 = held.tile([C, K - 1], F32, name="sumsq_123")
+        squares = [held.tile([C, D], F32, name=f"squares{k}") for k in range(K)]
+        nc.vector.scalar_tensor_tensor(
+            squares[0][:], cen[0][:], 1.0, cen[0][:], op0=ALU.mult, op1=ALU.mult, accum_out=sumsq_0[:]
+        )
+        for k in range(1, K):
+            nc.scalar.activation(squares[k][:], cen[k][:], ACT.Square, accum_out=sumsq_123[:, k - 1 : k])
 
         neg_cen_t = [held.tile([D, C], BF16, name=f"neg_cen_t{k}") for k in range(K)]
         for k in range(K):
-            cen_t = psum.tile([D, C], F32, name=f"cen_t{k}", tag=f"bank{k}")
+            cen_t = psum.tile([D, C], F32, name=f"cen_t{k}")
             nc.tensor.transpose(cen_t[:], cen[k][:], identity[:])
             nc.vector.tensor_scalar(neg_cen_t[k][:], cen_t[:], -1.0, None, op0=ALU.mult)
 
-        inv_length_0 = held.tile([C, 1], F32, name="inv_length_0", tag="inv_length_first")
-        nc.scalar.activation(inv_length_0[:], sumsq_v[0][:], ACT.Abs_reciprocal_sqrt)
-        inv_length_1 = held.tile([C, 1], F32, name="inv_length_1")
-        nc.scalar.activation(inv_length_1[:], sumsq_v[1][:], ACT.Abs_reciprocal_sqrt)
+        inv_length_0 = held.tile([C, 1], F32, name="inv_length_0")
+        nc.scalar.activation(inv_length_0[:], sumsq_0[:], ACT.Abs_reciprocal_sqrt)
+        inv_length_123 = held.tile([C, K - 1], F32, name="inv_length_123")
+        nc.scalar.activation(inv_length_123[:], sumsq_123[:], ACT.Abs_reciprocal_sqrt)
+        inv_length = [inv_length_0[:]] + [inv_length_123[:, k - 1 : k] for k in range(1, K)]
 
-        halves = [slice(0, N // 2), slice(N // 2, N)]
-        neg_dot = [
-            [psum.tile([C, N // 2], F32, name=f"neg_dot{k}{h}", tag=f"bank{(2 * k + h + 4) % 8}") for h in range(2)]
-            for k in range(K)
-        ]
-        for k, h in ((0, 0), (1, 0), (0, 1), (1, 1), (2, 0), (2, 1), (3, 0), (3, 1)):
-            nc.tensor.matmul(neg_dot[k][h][:], neg_cen_t[k][:], codes_sb[:, halves[h]], start=True, stop=True)
+        H, Q = N // 2, N // 4
+        halves = [slice(0, H), slice(H, N)]
+        half_dot = [[psum.tile([C, H], F32, name=f"half_dot{k}{h}") for h in range(2)] for k in range(2)]
+        whole_dot = [psum.tile([C, N], F32, name=f"whole_dot{k}", tag=f"cen_t{k - 2}") for k in (2, 3)]
+        for k in range(2):
+            for h in range(2):
+                nc.tensor.matmul(half_dot[k][h][:], neg_cen_t[k][:], codes_sb[:, halves[h]], start=True, stop=True)
+        for k in (2, 3):
+            nc.tensor.matmul(whole_dot[k - 2][:], neg_cen_t[k][:], codes_sb[:], start=True, stop=True)
+        quarters = [slice(q * Q, (q + 1) * Q) for q in range(4)]
+        neg_dot = [[half_dot[k][q // 2][:, quarters[q % 2]] for q in range(4)] for k in range(2)]
+        neg_dot += [[whole_dot[k - 2][:, quarters[q]] for q in range(4)] for k in (2, 3)]
 
-        Q = N // 4
         so_far = [held.tile([C, N], F32, name=f"so_far{k}") for k in range(K)]
         for q in range(4):
-            in_half = slice(q % 2 * Q, (q % 2 + 1) * Q)
-            nc.scalar.activation(
-                so_far[0][:, q * Q : (q + 1) * Q], neg_dot[0][q // 2][:, in_half], ACT.Copy, scale=inv_length_0[:]
-            )
-        inv_length_23 = held.tile([C, 2], F32, name="inv_length_23", tag="inv_length_first")
-        nc.scalar.activation(inv_length_23[:], sumsq_s[:], ACT.Abs_reciprocal_sqrt)
-        inv_length = {1: inv_length_1[:], 2: inv_length_23[:, 0:1], 3: inv_length_23[:, 1:2]}
+            nc.scalar.activation(so_far[0][:, quarters[q]], neg_dot[0][q], ACT.Copy, scale=inv_length[0])
         for k in range(1, K):
             for q in range(4):
-                quarter = slice(q * Q, (q + 1) * Q)
-                in_half = slice(q % 2 * Q, (q % 2 + 1) * Q)
                 nc.vector.scalar_tensor_tensor(
-                    so_far[k][:, quarter], neg_dot[k][q // 2][:, in_half], inv_length[k], so_far[k - 1][:, quarter],
+                    so_far[k][:, quarters[q]], neg_dot[k][q], inv_length[k], so_far[k - 1][:, quarters[q]],
                     op0=ALU.mult, op1=ALU.min,
                 )
         neg_max = so_far[K - 1]

@@ -29,11 +29,6 @@ def tile_cosinecodebook_kernel(tc, base, codes, centroids, offs, out):
         ones = held.tile([C, N], F32, name="ones")
         nc.gpsimd.memset(ones[:], 1.0)
 
-        warm_in = held.tile([C, 1], F32, name="warm_in")
-        nc.vector.memset(warm_in[:], 1.0)
-        warm = held.tile([C, 1], F32, name="warm")
-        nc.scalar.activation(warm[:], warm_in[:], ACT.Abs_reciprocal_sqrt)
-
         sumsq_0 = held.tile([C, 1], F32, name="sumsq_0")
         sumsq_123 = held.tile([C, K - 1], F32, name="sumsq_123")
         squares = [held.tile([C, D], F32, name=f"squares{k}") for k in range(K)]

import concourse.mybir as mybir
from concourse.masks import make_identity

C, K, D, S, N = 128, 4, 128, 512, 256
FLOPS = 2 * C * K * D * N

F32, BF16, U16 = mybir.dt.float32, mybir.dt.bfloat16, mybir.dt.uint16
ALU = mybir.AluOpType
ACT = mybir.ActivationFunctionType


def tile_cosinecodebook_kernel(tc, base, codes, centroids, offs, out):
    nc = tc.nc
    with tc.tile_pool(name="held", bufs=1) as held, tc.psum_pool(name="psum", bufs=1) as psum:
        cen = [held.tile([C, D], F32, name=f"cen{k}") for k in range(K)]
        nc.sync.dma_start(cen[0][:], centroids[:, 0, :])
        nc.sync.dma_start(cen[1][:], centroids[:, 1, :])
        nc.sync.dma_start(cen[2][:], centroids[:, 2, :])
        nc.sync.dma_start(cen[3][:], centroids[:, 3, :])
        codes_sb = held.tile([D, N], BF16, name="codes_sb")
        nc.sync.dma_start(codes_sb[:], codes)
        offsets = held.tile([C, N // 16], U16, name="offsets")
        nc.sync.dma_start(offsets[:], offs)
        bank = held.tile([C, S], F32, name="bank")
        nc.sync.dma_start(bank[:], base)

        identity = held.tile([C, C], F32, name="identity")
        make_identity(nc, identity[:])
        ones = held.tile([C, N], F32, name="ones")
        nc.gpsimd.memset(ones[:], 1.0)

        sumsq_0 = held.tile([C, 1], F32, name="sumsq_0")
        sumsq_123 = held.tile([C, K - 1], F32, name="sumsq_123")
        squares = [held.tile([C, D], F32, name=f"squares{k}") for k in range(K)]
        nc.vector.scalar_tensor_tensor(
            squares[0][:], cen[0][:], 1.0, cen[0][:], op0=ALU.mult, op1=ALU.mult, accum_out=sumsq_0[:]
        )
        for k in range(1, K):
            nc.scalar.activation(squares[k][:], cen[k][:], ACT.Square, accum_out=sumsq_123[:, k - 1 : k])

        neg_cen_t = [held.tile([D, C], BF16, name=f"neg_cen_t{k}") for k in range(K)]
        for k in range(K):
            cen_t = psum.tile([D, C], F32, name=f"cen_t{k}")
            nc.tensor.transpose(cen_t[:], cen[k][:], identity[:])
            nc.vector.tensor_scalar(neg_cen_t[k][:], cen_t[:], -1.0, None, op0=ALU.mult)

        inv_length_0 = held.tile([C, 1], F32, name="inv_length_0")
        nc.scalar.activation(inv_length_0[:], sumsq_0[:], ACT.Abs_reciprocal_sqrt)
        inv_length_123 = held.tile([C, K - 1], F32, name="inv_length_123")
        nc.scalar.activation(inv_length_123[:], sumsq_123[:], ACT.Abs_reciprocal_sqrt)
        inv_length = [inv_length_0[:]] + [inv_length_123[:, k - 1 : k] for k in range(1, K)]

        H, Q = N // 2, N // 4
        halves = [slice(0, H), slice(H, N)]
        half_dot = [[psum.tile([C, H], F32, name=f"half_dot{k}{h}") for h in range(2)] for k in range(2)]
        whole_dot = [psum.tile([C, N], F32, name=f"whole_dot{k}", tag=f"cen_t{k - 2}") for k in (2, 3)]
        for k in range(2):
            for h in range(2):
                nc.tensor.matmul(half_dot[k][h][:], neg_cen_t[k][:], codes_sb[:, halves[h]], start=True, stop=True)
        for k in (2, 3):
            nc.tensor.matmul(whole_dot[k - 2][:], neg_cen_t[k][:], codes_sb[:], start=True, stop=True)
        quarters = [slice(q * Q, (q + 1) * Q) for q in range(4)]
        neg_dot = [[half_dot[k][q // 2][:, quarters[q % 2]] for q in range(4)] for k in range(2)]
        neg_dot += [[whole_dot[k - 2][:, quarters[q]] for q in range(4)] for k in (2, 3)]

        so_far = [held.tile([C, N], F32, name=f"so_far{k}") for k in range(K)]
        for q in range(4):
            nc.scalar.activation(so_far[0][:, quarters[q]], neg_dot[0][q], ACT.Copy, scale=inv_length[0])
        for k in range(1, K):
            for q in range(4):
                nc.vector.scalar_tensor_tensor(
                    so_far[k][:, quarters[q]], neg_dot[k][q], inv_length[k], so_far[k - 1][:, quarters[q]],
                    op0=ALU.mult, op1=ALU.min,
                )
        neg_max = so_far[K - 1]

        nc.vector.tensor_tensor(bank[:].indirect(offsets[:]), ones[:], neg_max[:], ALU.add)
        nc.sync.dma_start(out, bank[:])
